import numpy as np
import ml_dtypes


def mxq(x, axis, fmt="e4m3"):
    dtype, down = {"e4m3": (ml_dtypes.float8_e4m3fn, 7), "e5m2": (ml_dtypes.float8_e5m2, 14)}[fmt]
    v = np.moveaxis(np.asarray(x, np.float32).astype(ml_dtypes.bfloat16).astype(np.float64), axis, -1)
    blocks = v.reshape(v.shape[:-1] + (-1, 32))
    amax = np.abs(blocks).max(-1, keepdims=True)
    byte = np.maximum(np.where(amax > 0, np.frexp(amax)[1] - 1 + 127, 0) - down, 1)
    scale = np.exp2(byte - 127.0)
    codes = (blocks / scale).astype(np.float32).astype(dtype).astype(np.float64)
    return np.moveaxis((codes * scale).reshape(v.shape), -1, axis)


WIDE = False


def mx_kscale(k):
    if not WIDE:
        return np.ones(k)
    levels = np.array([10, -10, 5, -5, 0])
    a = np.random.permutation(np.resize(levels, k // 512 * 4)).reshape(k // 512, 4)
    idx = np.arange(k)
    return np.exp2(a[idx // 512, idx % 128 // 32])


BF16 = ml_dtypes.bfloat16


def bf(x):
    return np.asarray(x, np.float32).astype(BF16)


def f64(x):
    return np.asarray(x).astype(np.float64)


LMAX, MMAX, C_IN, C_OUT, E, D_EMB = 6, 2, 512, 128, 256, 8
M_SIZE = [LMAX + 1] + [LMAX - m + 1 for m in range(1, MMAX + 1)]
NUM_COEFFS = M_SIZE[0] + 2 * sum(M_SIZE[1:])
K0, K1, K2 = M_SIZE[0] * C_IN, M_SIZE[1] * C_IN, M_SIZE[2] * C_IN


def setup_inputs():
    s0, s1, s2 = mx_kscale(K0), mx_kscale(K1), mx_kscale(K2)
    s = np.concatenate([s0.reshape(-1, C_IN), s1.reshape(-1, C_IN), s1.reshape(-1, C_IN), s2.reshape(-1, C_IN), s2.reshape(-1, C_IN)], axis=0)
    return {"edge_feats": bf(np.random.standard_normal((E, NUM_COEFFS, C_IN)) * s[None, :, :]),
            "edge_embeds": bf(np.random.standard_normal((E, D_EMB))),
            "W0": bf(np.random.standard_normal((K0, M_SIZE[0] * C_OUT)) / np.sqrt(K0) / s0[:, None]),
            "b0": bf(np.random.standard_normal(M_SIZE[0] * C_OUT) * 0.3),
            "W1": bf(np.random.standard_normal((K1, 2 * M_SIZE[1] * C_OUT)) / np.sqrt(K1) / s1[:, None]),
            "W2": bf(np.random.standard_normal((K2, 2 * M_SIZE[2] * C_OUT)) / np.sqrt(K2) / s2[:, None])}


def reference(edge_feats, edge_embeds, W0, b0, W1, W2):
    edge_feats = f64(edge_feats)
    num_edges = f64(edge_embeds).shape[0]
    feats_0 = edge_feats[:, :M_SIZE[0]].reshape(num_edges, -1)
    feats_0 = (mxq(feats_0, 1, "e4m3") @ mxq(f64(W0), 0, "e4m3")) + f64(b0)
    feats_out = [feats_0.reshape(num_edges, -1, C_OUT)]
    offset = M_SIZE[0]
    Wm_list = [f64(W1), f64(W2)]
    for m in range(1, MMAX + 1):
        feats_m = edge_feats[:, offset:offset + 2 * M_SIZE[m]].reshape(num_edges, 2, -1)
        offset += 2 * M_SIZE[m]
        feats_m = mxq(feats_m, 2, "e4m3") @ mxq(Wm_list[m - 1], 0, "e4m3")
        feats_r, feats_i = np.split(feats_m, 2, axis=2)
        feats_m_r = feats_r[:, 0] - feats_i[:, 1]
        feats_m_i = feats_r[:, 1] + feats_i[:, 0]
        feats_out.append(feats_m_r.reshape(num_edges, -1, C_OUT))
        feats_out.append(feats_m_i.reshape(num_edges, -1, C_OUT))
    return np.concatenate(feats_out, axis=1)

@@ -1,0 +1,168 @@
+from contextlib import ExitStack
+
+import concourse.mybir as mybir
+from concourse.masks import make_identity
+
+F32 = mybir.dt.float32
+BF16 = mybir.dt.bfloat16
+U32 = mybir.dt.uint32
+U8 = mybir.dt.uint8
+FP8X4 = mybir.dt.float8_e4m3fn_x4
+
+P = 128
+PACK = 4
+K_PASS = P * PACK
+C_OUT = 128
+EDGE_TILES = 2
+BANK = 512
+LOAD_COEFFS = 4
+
+FLOPS = 2 * 256 * (3584 * 896 + 2 * 3072 * 1536 + 2 * 2560 * 1280)
+
+
+def power_of_two_pieces(width, largest):
+    pieces = []
+    start = 0
+    size = largest
+    while start < width:
+        while size > width - start:
+            size = size // 2
+        pieces.append((start, size))
+        start += size
+    return pieces
+
+
+def tile_so2convolution_kernel(tc, edge_feats, edge_embeds, W0, b0, W1, W2, out):
+    nc = tc.nc
+    orders = [(W1, 7, 6, True), (W2, 19, 5, True), (W0, 0, 7, False)]
+
+    with ExitStack() as ctx:
+        const = ctx.enter_context(tc.tile_pool(name="const", bufs=1))
+        feats = ctx.enter_context(tc.tile_pool(name="feats", bufs=1))
+        xload = ctx.enter_context(tc.tile_pool(name="xload", bufs=3))
+        xwork = ctx.enter_context(tc.tile_pool(name="xwork", bufs=4))
+        wload = ctx.enter_context(tc.tile_pool(name="wload", bufs=4))
+        wwork = ctx.enter_context(tc.tile_pool(name="wwork", bufs=3))
+        wquant = ctx.enter_context(tc.tile_pool(name="wquant", bufs=4))
+        result = ctx.enter_context(tc.tile_pool(name="result", bufs=3))
+        psum = ctx.enter_context(tc.psum_pool(name="psum", bufs=8))
+
+        identity = const.tile([P, P], F32)
+        make_identity(nc, identity[:])
+        bias = const.tile([P, 7 * C_OUT], BF16)
+        nc.gpsimd.dma_start(out=bias[:], in_=b0.partition_broadcast(P))
+
+        x_codes = {}
+        x_scales = {}
+        neg_codes = {}
+        neg_scales = {}
+        for weight, first, count, is_complex in orders:
+            groups = 2 if is_complex else 1
+            last = first + groups * count
+            for c0 in range(first, last, LOAD_COEFFS):
+                n_coeffs = min(LOAD_COEFFS, last - c0)
+                xraw = xload.tile([P, EDGE_TILES * n_coeffs * K_PASS], BF16)
+                nc.sync.dma_start(
+                    out=xraw[:].rearrange("p (t x) -> p t x", t=EDGE_TILES),
+                    in_=edge_feats[:, c0 : c0 + n_coeffs, :].rearrange("(t p) c k -> p t (c k)", p=P),
+                )
+                xwords = xraw[:].bitcast(F32)
+                for j in range(n_coeffs):
+                    c = c0 + j
+                    bank = psum.tile([P, BANK], F32, tag="bank")
+                    for t in range(EDGE_TILES):
+                        for u in range(2):
+                            w0 = ((t * n_coeffs + j) * 2 + u) * P
+                            s = 2 * t + u
+                            nc.tensor.transpose(bank[:, s * P : (s + 1) * P], xwords[:, w0 : w0 + P], identity[:])
+                    xg = xwork.tile([P, EDGE_TILES * P * PACK], BF16, align_bytes=64)
+                    nc.scalar.copy(
+                        out=xg[:].bitcast(F32).rearrange("p (t e u) -> p t e u", t=EDGE_TILES, u=2),
+                        in_=bank[:].rearrange("p (t u e) -> p t e u", t=EDGE_TILES, u=2),
+                    )
+                    x_codes[c] = feats.tile([P, EDGE_TILES * P], U32, name="xq%d" % c, align_bytes=64)
+                    x_scales[c] = feats.tile([P, EDGE_TILES * P], U8, name="xs%d" % c, align_bytes=64)
+                    nc.vector.quantize_mx(out=x_codes[c][:].bitcast(FP8X4), scales=x_scales[c][:], in_=xg[:])
+                    if is_complex and c >= first + count:
+                        xn = xwork.tile([P, EDGE_TILES * P * PACK], BF16, align_bytes=64)
+                        nc.vector.tensor_scalar_mul(out=xn[:], in0=xg[:], scalar1=-1.0)
+                        neg_codes[c] = feats.tile([P, EDGE_TILES * P], U32, name="nq%d" % c, align_bytes=64)
+                        neg_scales[c] = feats.tile([P, EDGE_TILES * P], U8, name="ns%d" % c, align_bytes=64)
+                        nc.vector.quantize_mx(out=neg_codes[c][:].bitcast(FP8X4), scales=neg_scales[c][:], in_=xn[:])
+
+        for weight, first, count, is_complex in orders:
+            width = count * C_OUT
+            n_cols = weight.shape[1]
+            parts = 2 if is_complex else 1
+            chunks = power_of_two_pieces(width, BANK)
+            acc = {}
+            for t in range(EDGE_TILES):
+                for part in range(parts):
+                    for a, w in chunks:
+                        acc[(t, part, a)] = psum.tile([P, BANK], F32, tag="bank", name="acc_%d_%d_%d_%d" % (first, t, part, a))
+            for g in range(count):
+                wraw = wload.tile([P, PACK, n_cols], BF16)
+                nc.sync.dma_start(
+                    out=wraw[:].rearrange("p (u e) n -> p u e n", u=2),
+                    in_=weight[g * K_PASS : (g + 1) * K_PASS, :].rearrange("(u p e) n -> p u e n", u=2, e=2),
+                )
+                wg = wwork.tile([P, n_cols, PACK], BF16, align_bytes=64)
+                half = n_cols // 2
+                nc.vector.tensor_copy(
+                    out=wg[:, 0:half, :].rearrange("p (c i) t -> p c t i", i=4),
+                    in_=wraw[:, :, 0:half].rearrange("p t (c i) -> p c t i", i=4),
+                )
+                nc.scalar.copy(
+                    out=wg[:, half:n_cols, :].rearrange("p (c i) t -> p c t i", i=4),
+                    in_=wraw[:, :, half:n_cols].rearrange("p t (c i) -> p c t i", i=4),
+                )
+                wq = wquant.tile([P, n_cols], U32, align_bytes=64)
+                ws = wquant.tile([P, n_cols], U8, align_bytes=64)
+                for a, w in power_of_two_pieces(n_cols, 1024):
+                    nc.vector.quantize_mx(
+                        out=wq[:, a : a + w].bitcast(FP8X4),
+                        scales=ws[:, a : a + w],
+                        in_=wg[:, a : a + w, :].rearrange("p w j -> p (w j)"),
+                    )
+                re = first + g
+                im = first + count + g
+                for t in range(EDGE_TILES):
+                    edges = slice(t * P, (t + 1) * P)
+                    for part in range(parts):
+                        if not is_complex:
+                            terms = [(x_codes[re], x_scales[re], 0)]
+                        elif part == 0:
+                            terms = [(x_codes[re], x_scales[re], 0), (neg_codes[im], neg_scales[im], width)]
+                        else:
+                            terms = [(x_codes[im], x_scales[im], 0), (x_codes[re], x_scales[re], width)]
+                        for a, w in chunks:
+                            for i, (codes, scales, offset) in enumerate(terms):
+                                cols = slice(offset + a, offset + a + w)
+                                nc.tensor.matmul_mx(
+                                    out=acc[(t, part, a)][:, 0:w],
+                                    lhsT=codes[:, edges].bitcast(FP8X4),
+                                    lhsT_scale=scales[:, edges],
+                                    rhs=wq[:, cols].bitcast(FP8X4),
+                                    rhs_scale=ws[:, cols],
+                                    start=(g == 0 and i == 0),
+                                    stop=(g == count - 1 and i == len(terms) - 1),
+                                )
+            for t in range(EDGE_TILES):
+                for part in range(parts):
+                    stage = result.tile([P, width], F32)
+                    for a, w in chunks:
+                        if is_complex:
+                            nc.scalar.copy(out=stage[:, a : a + w], in_=acc[(t, part, a)][:, 0:w])
+                        else:
+                            nc.vector.tensor_tensor(
+                                out=stage[:, a : a + w],
+                                in0=acc[(t, part, a)][:, 0:w],
+                                in1=bias[:, a : a + w],
+                                op=mybir.AluOpType.add,
+                            )
+                    c0 = first + part * count
+                    target = out[t * P : (t + 1) * P, c0 : c0 + count, :].rearrange("p c d -> p (c d)")
+                    if is_complex:
+                        nc.scalar.dma_start(out=target, in_=stage[:])
+                    else:
+                        nc.sync.dma_start(out=target, in_=stage[:])

@@ -16,6 +16,7 @@ C_OUT = 128
 EDGE_TILES = 2
 BANK = 512
 LOAD_COEFFS = 4
+RAW_PASSES = 4
 
 FLOPS = 2 * 256 * (3584 * 896 + 2 * 3072 * 1536 + 2 * 2560 * 1280)
 
@@ -35,134 +36,189 @@ def power_of_two_pieces(width, largest):
 def tile_so2convolution_kernel(tc, edge_feats, edge_embeds, W0, b0, W1, W2, out):
     nc = tc.nc
     orders = [(W1, 7, 6, True), (W2, 19, 5, True), (W0, 0, 7, False)]
+    passes = []
+    imaginary = []
+    for m, (weight, first, count, is_complex) in enumerate(orders):
+        passes.extend([(m, g) for g in range(count)])
+        if is_complex:
+            imaginary.extend(range(first + count, first + 2 * count))
 
     with ExitStack() as ctx:
+        ctx.enter_context(tc.manual_schedule())
         const = ctx.enter_context(tc.tile_pool(name="const", bufs=1))
         feats = ctx.enter_context(tc.tile_pool(name="feats", bufs=1))
         xload = ctx.enter_context(tc.tile_pool(name="xload", bufs=3))
         xwork = ctx.enter_context(tc.tile_pool(name="xwork", bufs=4))
-        wload = ctx.enter_context(tc.tile_pool(name="wload", bufs=4))
+        wload = ctx.enter_context(tc.tile_pool(name="wload", bufs=RAW_PASSES))
         wwork = ctx.enter_context(tc.tile_pool(name="wwork", bufs=3))
         wquant = ctx.enter_context(tc.tile_pool(name="wquant", bufs=4))
-        result = ctx.enter_context(tc.tile_pool(name="result", bufs=3))
+        result = ctx.enter_context(tc.tile_pool(name="result", bufs=6))
         psum = ctx.enter_context(tc.psum_pool(name="psum", bufs=8))
 
         identity = const.tile([P, P], F32)
         make_identity(nc, identity[:])
-        bias = const.tile([P, 7 * C_OUT], BF16)
-        nc.gpsimd.dma_start(out=bias[:], in_=b0.partition_broadcast(P))
+
+        ones = const.tile([P, P], BF16)
+        nc.vector.memset(ones[:], 1.0)
+        bias_row = const.tile([P, 2 * BANK], BF16)
+        nc.vector.memset(bias_row[:], 0.0)
+        nc.scalar.dma_start(out=bias_row[0:1, 0 : 7 * C_OUT], in_=b0.rearrange("(o n) -> o n", o=1))
 
         x_codes = {}
         x_scales = {}
         neg_codes = {}
         neg_scales = {}
-        for weight, first, count, is_complex in orders:
-            groups = 2 if is_complex else 1
-            last = first + groups * count
-            for c0 in range(first, last, LOAD_COEFFS):
-                n_coeffs = min(LOAD_COEFFS, last - c0)
-                xraw = xload.tile([P, EDGE_TILES * n_coeffs * K_PASS], BF16)
-                nc.sync.dma_start(
-                    out=xraw[:].rearrange("p (t x) -> p t x", t=EDGE_TILES),
-                    in_=edge_feats[:, c0 : c0 + n_coeffs, :].rearrange("(t p) c k -> p t (c k)", p=P),
-                )
-                xwords = xraw[:].bitcast(F32)
-                for j in range(n_coeffs):
-                    c = c0 + j
-                    bank = psum.tile([P, BANK], F32, tag="bank")
-                    for t in range(EDGE_TILES):
-                        for u in range(2):
-                            w0 = ((t * n_coeffs + j) * 2 + u) * P
-                            s = 2 * t + u
-                            nc.tensor.transpose(bank[:, s * P : (s + 1) * P], xwords[:, w0 : w0 + P], identity[:])
-                    xg = xwork.tile([P, EDGE_TILES * P * PACK], BF16, align_bytes=64)
-                    nc.scalar.copy(
-                        out=xg[:].bitcast(F32).rearrange("p (t e u) -> p t e u", t=EDGE_TILES, u=2),
-                        in_=bank[:].rearrange("p (t u e) -> p t e u", t=EDGE_TILES, u=2),
-                    )
-                    x_codes[c] = feats.tile([P, EDGE_TILES * P], U32, name="xq%d" % c, align_bytes=64)
-                    x_scales[c] = feats.tile([P, EDGE_TILES * P], U8, name="xs%d" % c, align_bytes=64)
-                    nc.vector.quantize_mx(out=x_codes[c][:].bitcast(FP8X4), scales=x_scales[c][:], in_=xg[:])
-                    if is_complex and c >= first + count:
-                        xn = xwork.tile([P, EDGE_TILES * P * PACK], BF16, align_bytes=64)
-                        nc.vector.tensor_scalar_mul(out=xn[:], in0=xg[:], scalar1=-1.0)
-                        neg_codes[c] = feats.tile([P, EDGE_TILES * P], U32, name="nq%d" % c, align_bytes=64)
-                        neg_scales[c] = feats.tile([P, EDGE_TILES * P], U8, name="ns%d" % c, align_bytes=64)
-                        nc.vector.quantize_mx(out=neg_codes[c][:].bitcast(FP8X4), scales=neg_scales[c][:], in_=xn[:])
-
-        for weight, first, count, is_complex in orders:
-            width = count * C_OUT
-            n_cols = weight.shape[1]
-            parts = 2 if is_complex else 1
-            chunks = power_of_two_pieces(width, BANK)
-            acc = {}
-            for t in range(EDGE_TILES):
-                for part in range(parts):
-                    for a, w in chunks:
-                        acc[(t, part, a)] = psum.tile([P, BANK], F32, tag="bank", name="acc_%d_%d_%d_%d" % (first, t, part, a))
-            for g in range(count):
-                wraw = wload.tile([P, PACK, n_cols], BF16)
-                nc.sync.dma_start(
-                    out=wraw[:].rearrange("p (u e) n -> p u e n", u=2),
-                    in_=weight[g * K_PASS : (g + 1) * K_PASS, :].rearrange("(u p e) n -> p u e n", u=2, e=2),
-                )
-                wg = wwork.tile([P, n_cols, PACK], BF16, align_bytes=64)
-                half = n_cols // 2
-                nc.vector.tensor_copy(
-                    out=wg[:, 0:half, :].rearrange("p (c i) t -> p c t i", i=4),
-                    in_=wraw[:, :, 0:half].rearrange("p t (c i) -> p c t i", i=4),
-                )
-                nc.scalar.copy(
-                    out=wg[:, half:n_cols, :].rearrange("p (c i) t -> p c t i", i=4),
-                    in_=wraw[:, :, half:n_cols].rearrange("p t (c i) -> p c t i", i=4),
-                )
-                wq = wquant.tile([P, n_cols], U32, align_bytes=64)
-                ws = wquant.tile([P, n_cols], U8, align_bytes=64)
-                for a, w in power_of_two_pieces(n_cols, 1024):
-                    nc.vector.quantize_mx(
-                        out=wq[:, a : a + w].bitcast(FP8X4),
-                        scales=ws[:, a : a + w],
-                        in_=wg[:, a : a + w, :].rearrange("p w j -> p (w j)"),
-                    )
-                re = first + g
-                im = first + count + g
+        loads = []
+        load_size = 1
+        for first, last in [(7, 29), (0, 7)]:
+            c0 = first
+            while c0 < last:
+                n_coeffs = min(load_size, last - c0)
+                loads.append((c0, n_coeffs))
+                c0 += n_coeffs
+                load_size = min(2 * load_size, LOAD_COEFFS)
+        for c0, n_coeffs in loads:
+            xraw = xload.tile([P, EDGE_TILES * n_coeffs * K_PASS], BF16)
+            nc.sync.dma_start(
+                out=xraw[:].rearrange("p (t x) -> p t x", t=EDGE_TILES),
+                in_=edge_feats[:, c0 : c0 + n_coeffs, :].rearrange("(t p) c k -> p t (c k)", p=P),
+            )
+            xwords = xraw[:].bitcast(F32)
+            for j in range(n_coeffs):
+                c = c0 + j
+                bank = psum.tile([P, BANK], F32, tag="bank")
                 for t in range(EDGE_TILES):
-                    edges = slice(t * P, (t + 1) * P)
-                    for part in range(parts):
-                        if not is_complex:
-                            terms = [(x_codes[re], x_scales[re], 0)]
-                        elif part == 0:
-                            terms = [(x_codes[re], x_scales[re], 0), (neg_codes[im], neg_scales[im], width)]
-                        else:
-                            terms = [(x_codes[im], x_scales[im], 0), (x_codes[re], x_scales[re], width)]
-                        for a, w in chunks:
-                            for i, (codes, scales, offset) in enumerate(terms):
-                                cols = slice(offset + a, offset + a + w)
-                                nc.tensor.matmul_mx(
-                                    out=acc[(t, part, a)][:, 0:w],
-                                    lhsT=codes[:, edges].bitcast(FP8X4),
-                                    lhsT_scale=scales[:, edges],
-                                    rhs=wq[:, cols].bitcast(FP8X4),
-                                    rhs_scale=ws[:, cols],
-                                    start=(g == 0 and i == 0),
-                                    stop=(g == count - 1 and i == len(terms) - 1),
-                                )
+                    for u in range(2):
+                        w0 = ((t * n_coeffs + j) * 2 + u) * P
+                        s = 2 * t + u
+                        nc.tensor.transpose(bank[:, s * P : (s + 1) * P], xwords[:, w0 : w0 + P], identity[:])
+                xg = xwork.tile([P, EDGE_TILES * P * PACK], BF16, align_bytes=64)
+                nc.scalar.copy(
+                    out=xg[:].bitcast(F32).rearrange("p (t e u) -> p t e u", t=EDGE_TILES, u=2),
+                    in_=bank[:].rearrange("p (t u e) -> p t e u", t=EDGE_TILES, u=2),
+                )
+                if c in imaginary:
+                    xn = xwork.tile([P, EDGE_TILES * P * PACK], BF16, align_bytes=64)
+                    nc.vector.tensor_scalar_mul(out=xn[:], in0=xg[:], scalar1=-1.0)
+                x_codes[c] = feats.tile([P, EDGE_TILES * P], U32, name="xq%d" % c, align_bytes=64)
+                x_scales[c] = feats.tile([P, EDGE_TILES * P], U8, name="xs%d" % c, align_bytes=64)
+                nc.vector.quantize_mx(out=x_codes[c][:].bitcast(FP8X4), scales=x_scales[c][:], in_=xg[:])
+                if c in imaginary:
+                    neg_codes[c] = feats.tile([P, EDGE_TILES * P], U32, name="nq%d" % c, align_bytes=64)
+                    neg_scales[c] = feats.tile([P, EDGE_TILES * P], U8, name="ns%d" % c, align_bytes=64)
+                    nc.vector.quantize_mx(out=neg_codes[c][:].bitcast(FP8X4), scales=neg_scales[c][:], in_=xn[:])
+
+        bias = const.tile([P, 2 * BANK], F32)
+        for a in range(0, 2 * BANK, BANK):
+            spread = psum.tile([P, BANK], F32, tag="bank")
+            nc.tensor.matmul(spread[:], lhsT=ones[:], rhs=bias_row[:, a : a + BANK], start=True, stop=True)
+            nc.vector.tensor_copy(out=bias[:, a : a + BANK], in_=spread[:])
+
+        raw = {}
+        grouped = {}
+        w_codes = {}
+        w_scales = {}
+        acc = {}
+
+        def load(i):
+            m, g = passes[i]
+            weight = orders[m][0]
+            raw[i] = wload.tile([P, PACK, weight.shape[1]], BF16, name="wraw%d" % i, tag="wraw")
+            nc.sync.dma_start(
+                out=raw[i][:].rearrange("p (u e) n -> p u e n", u=2),
+                in_=weight[g * K_PASS : (g + 1) * K_PASS, :].rearrange("(u p e) n -> p u e n", u=2, e=2),
+            )
+
+        def regroup(i):
+            n_cols = orders[passes[i][0]][0].shape[1]
+            half = n_cols // 2
+            grouped[i] = wwork.tile([P, n_cols, PACK], BF16, name="wg%d" % i, tag="wg", align_bytes=64)
+            nc.vector.tensor_copy(
+                out=grouped[i][:, 0:half, :].rearrange("p (c i) t -> p c t i", i=4),
+                in_=raw[i][:, :, 0:half].rearrange("p t (c i) -> p c t i", i=4),
+            )
+            nc.scalar.copy(
+                out=grouped[i][:, half:n_cols, :].rearrange("p (c i) t -> p c t i", i=4),
+                in_=raw[i][:, :, half:n_cols].rearrange("p t (c i) -> p c t i", i=4),
+            )
+
+        def quantise(i):
+            n_cols = orders[passes[i][0]][0].shape[1]
+            w_codes[i] = wquant.tile([P, n_cols], U32, name="wq%d" % i, tag="wq", align_bytes=64)
+            w_scales[i] = wquant.tile([P, n_cols], U8, name="ws%d" % i, tag="ws", align_bytes=64)
+            for a, w in power_of_two_pieces(n_cols, 1024):
+                nc.vector.quantize_mx(
+                    out=w_codes[i][:, a : a + w].bitcast(FP8X4),
+                    scales=w_scales[i][:, a : a + w],
+                    in_=grouped[i][:, a : a + w, :].rearrange("p w j -> p (w j)"),
+                )
+
+        def multiply(i):
+            m, g = passes[i]
+            weight, first, count, is_complex = orders[m]
+            width = count * C_OUT
+            re = first + g
+            im = first + count + g
             for t in range(EDGE_TILES):
-                for part in range(parts):
+                edges = slice(t * P, (t + 1) * P)
+                for part in range(2 if is_complex else 1):
+                    if not is_complex:
+                        terms = [(x_codes[re], x_scales[re], 0)]
+                    elif part == 0:
+                        terms = [(x_codes[re], x_scales[re], 0), (neg_codes[im], neg_scales[im], width)]
+                    else:
+                        terms = [(x_codes[im], x_scales[im], 0), (x_codes[re], x_scales[re], width)]
+                    for a, w in power_of_two_pieces(width, BANK):
+                        if g == 0:
+                            acc[(m, t, part, a)] = psum.tile([P, BANK], F32, tag="bank", name="acc_%d_%d_%d_%d" % (m, t, part, a))
+                        for k, (codes, scales, offset) in enumerate(terms):
+                            cols = slice(offset + a, offset + a + w)
+                            nc.tensor.matmul_mx(
+                                out=acc[(m, t, part, a)][:, 0:w],
+                                lhsT=codes[:, edges].bitcast(FP8X4),
+                                lhsT_scale=scales[:, edges],
+                                rhs=w_codes[i][:, cols].bitcast(FP8X4),
+                                rhs_scale=w_scales[i][:, cols],
+                                start=(g == 0 and k == 0),
+                                stop=(g == count - 1 and k == len(terms) - 1),
+                            )
+
+        def finish(m):
+            weight, first, count, is_complex = orders[m]
+            width = count * C_OUT
+            for t in range(EDGE_TILES):
+                for part in range(2 if is_complex else 1):
                     stage = result.tile([P, width], F32)
-                    for a, w in chunks:
-                        if is_complex:
-                            nc.scalar.copy(out=stage[:, a : a + w], in_=acc[(t, part, a)][:, 0:w])
-                        else:
+                    for a, w in power_of_two_pieces(width, BANK):
+                        if not is_complex:
                             nc.vector.tensor_tensor(
                                 out=stage[:, a : a + w],
-                                in0=acc[(t, part, a)][:, 0:w],
+                                in0=acc[(m, t, part, a)][:, 0:w],
                                 in1=bias[:, a : a + w],
                                 op=mybir.AluOpType.add,
                             )
+                        elif part == 0:
+                            nc.scalar.copy(out=stage[:, a : a + w], in_=acc[(m, t, part, a)][:, 0:w])
+                        else:
+                            nc.vector.tensor_copy(out=stage[:, a : a + w], in_=acc[(m, t, part, a)][:, 0:w])
                     c0 = first + part * count
-                    target = out[t * P : (t + 1) * P, c0 : c0 + count, :].rearrange("p c d -> p (c d)")
-                    if is_complex:
-                        nc.scalar.dma_start(out=target, in_=stage[:])
-                    else:
-                        nc.sync.dma_start(out=target, in_=stage[:])
+                    nc.sync.dma_start(
+                        out=out[t * P : (t + 1) * P, c0 : c0 + count, :].rearrange("p c d -> p (c d)"),
+                        in_=stage[:],
+                    )
+
+        for i in range(RAW_PASSES):
+            load(i)
+        for s in range(len(passes) + 2):
+            if s < len(passes):
+                regroup(s)
+            if s + RAW_PASSES < len(passes):
+                load(s + RAW_PASSES)
+            if 1 <= s <= len(passes):
+                quantise(s - 1)
+            if s >= 2:
+                m, g = passes[s - 2]
+                if g == orders[m][2] - 1:
+                    finish(m)
+            if 1 <= s <= len(passes):
+                multiply(s - 1)

@@ -51,8 +51,8 @@ def tile_so2convolution_kernel(tc, edge_feats, edge_embeds, W0, b0, W1, W2, out)
         xwork = ctx.enter_context(tc.tile_pool(name="xwork", bufs=4))
         wload = ctx.enter_context(tc.tile_pool(name="wload", bufs=RAW_PASSES))
         wwork = ctx.enter_context(tc.tile_pool(name="wwork", bufs=3))
-        wquant = ctx.enter_context(tc.tile_pool(name="wquant", bufs=4))
-        result = ctx.enter_context(tc.tile_pool(name="result", bufs=6))
+        wquant = ctx.enter_context(tc.tile_pool(name="wquant", bufs=3))
+        result = ctx.enter_context(tc.tile_pool(name="result", bufs=8))
         psum = ctx.enter_context(tc.psum_pool(name="psum", bufs=8))
 
         identity = const.tile([P, P], F32)
@@ -119,6 +119,7 @@ def tile_so2convolution_kernel(tc, edge_feats, edge_embeds, W0, b0, W1, W2, out)
         w_codes = {}
         w_scales = {}
         acc = {}
+        stores = []
 
         def load(i):
             m, g = passes[i]
@@ -202,10 +203,7 @@ def tile_so2convolution_kernel(tc, edge_feats, edge_embeds, W0, b0, W1, W2, out)
                         else:
                             nc.vector.tensor_copy(out=stage[:, a : a + w], in_=acc[(m, t, part, a)][:, 0:w])
                     c0 = first + part * count
-                    nc.sync.dma_start(
-                        out=out[t * P : (t + 1) * P, c0 : c0 + count, :].rearrange("p c d -> p (c d)"),
-                        in_=stage[:],
-                    )
+                    stores.append((out[t * P : (t + 1) * P, c0 : c0 + count, :].rearrange("p c d -> p (c d)"), stage))
 
         for i in range(RAW_PASSES):
             load(i)
@@ -222,3 +220,7 @@ def tile_so2convolution_kernel(tc, edge_feats, edge_embeds, W0, b0, W1, W2, out)
                     finish(m)
             if 1 <= s <= len(passes):
                 multiply(s - 1)
+            if s + RAW_PASSES >= len(passes) - 1:
+                for target, stage in stores:
+                    nc.sync.dma_start(out=target, in_=stage[:])
+                stores = []

@@ -15,8 +15,9 @@ K_PASS = P * PACK
 C_OUT = 128
 EDGE_TILES = 2
 BANK = 512
-LOAD_COEFFS = 4
+LOAD_COEFFS = 3
 RAW_PASSES = 4
+VECTOR_FEWER = 32
 
 FLOPS = 2 * 256 * (3584 * 896 + 2 * 3072 * 1536 + 2 * 2560 * 1280)
 
@@ -47,7 +48,7 @@ def tile_so2convolution_kernel(tc, edge_feats, edge_embeds, W0, b0, W1, W2, out)
         ctx.enter_context(tc.manual_schedule())
         const = ctx.enter_context(tc.tile_pool(name="const", bufs=1))
         feats = ctx.enter_context(tc.tile_pool(name="feats", bufs=1))
-        xload = ctx.enter_context(tc.tile_pool(name="xload", bufs=3))
+        xload = ctx.enter_context(tc.tile_pool(name="xload", bufs=4))
         xwork = ctx.enter_context(tc.tile_pool(name="xwork", bufs=4))
         wload = ctx.enter_context(tc.tile_pool(name="wload", bufs=RAW_PASSES))
         wwork = ctx.enter_context(tc.tile_pool(name="wwork", bufs=3))
@@ -70,12 +71,14 @@ def tile_so2convolution_kernel(tc, edge_feats, edge_embeds, W0, b0, W1, W2, out)
         neg_scales = {}
         loads = []
         load_size = 1
-        for first, last in [(7, 29), (0, 7)]:
-            c0 = first
-            while c0 < last:
-                n_coeffs = min(load_size, last - c0)
-                loads.append((c0, n_coeffs))
-                c0 += n_coeffs
+        for weight, first, count, is_complex in orders:
+            a = 0
+            while a < count:
+                n_coeffs = min(load_size, count - a)
+                if is_complex:
+                    loads.append((first + count + a, n_coeffs))
+                loads.append((first + a, n_coeffs))
+                a += n_coeffs
                 load_size = min(2 * load_size, LOAD_COEFFS)
         for c0, n_coeffs in loads:
             xraw = xload.tile([P, EDGE_TILES * n_coeffs * K_PASS], BF16)
@@ -112,7 +115,7 @@ def tile_so2convolution_kernel(tc, edge_feats, edge_embeds, W0, b0, W1, W2, out)
         for a in range(0, 2 * BANK, BANK):
             spread = psum.tile([P, BANK], F32, tag="bank")
             nc.tensor.matmul(spread[:], lhsT=ones[:], rhs=bias_row[:, a : a + BANK], start=True, stop=True)
-            nc.vector.tensor_copy(out=bias[:, a : a + BANK], in_=spread[:])
+            nc.scalar.copy(out=bias[:, a : a + BANK], in_=spread[:])
 
         raw = {}
         grouped = {}
@@ -132,15 +135,15 @@ def tile_so2convolution_kernel(tc, edge_feats, edge_embeds, W0, b0, W1, W2, out)
 
         def regroup(i):
             n_cols = orders[passes[i][0]][0].shape[1]
-            half = n_cols // 2
+            split = n_cols // 2 - VECTOR_FEWER
             grouped[i] = wwork.tile([P, n_cols, PACK], BF16, name="wg%d" % i, tag="wg", align_bytes=64)
             nc.vector.tensor_copy(
-                out=grouped[i][:, 0:half, :].rearrange("p (c i) t -> p c t i", i=4),
-                in_=raw[i][:, :, 0:half].rearrange("p t (c i) -> p c t i", i=4),
+                out=grouped[i][:, 0:split, :].rearrange("p (c i) t -> p c t i", i=4),
+                in_=raw[i][:, :, 0:split].rearrange("p t (c i) -> p c t i", i=4),
             )
             nc.scalar.copy(
-                out=grouped[i][:, half:n_cols, :].rearrange("p (c i) t -> p c t i", i=4),
-                in_=raw[i][:, :, half:n_cols].rearrange("p t (c i) -> p c t i", i=4),
+                out=grouped[i][:, split:n_cols, :].rearrange("p (c i) t -> p c t i", i=4),
+                in_=raw[i][:, :, split:n_cols].rearrange("p t (c i) -> p c t i", i=4),
             )
 
         def quantise(i):

from contextlib import ExitStack

import concourse.mybir as mybir
from concourse.masks import make_identity

F32 = mybir.dt.float32
BF16 = mybir.dt.bfloat16
U32 = mybir.dt.uint32
U8 = mybir.dt.uint8
FP8X4 = mybir.dt.float8_e4m3fn_x4

P = 128
PACK = 4
K_PASS = P * PACK
C_OUT = 128
EDGE_TILES = 2
BANK = 512
LOAD_COEFFS = 3
RAW_PASSES = 4
VECTOR_FEWER = 32

FLOPS = 2 * 256 * (3584 * 896 + 2 * 3072 * 1536 + 2 * 2560 * 1280)


def power_of_two_pieces(width, largest):
    pieces = []
    start = 0
    size = largest
    while start < width:
        while size > width - start:
            size = size // 2
        pieces.append((start, size))
        start += size
    return pieces


def tile_so2convolution_kernel(tc, edge_feats, edge_embeds, W0, b0, W1, W2, out):
    nc = tc.nc
    orders = [(W1, 7, 6, True), (W2, 19, 5, True), (W0, 0, 7, False)]
    passes = []
    imaginary = []
    for m, (weight, first, count, is_complex) in enumerate(orders):
        passes.extend([(m, g) for g in range(count)])
        if is_complex:
            imaginary.extend(range(first + count, first + 2 * count))

    with ExitStack() as ctx:
        ctx.enter_context(tc.manual_schedule())
        const = ctx.enter_context(tc.tile_pool(name="const", bufs=1))
        feats = ctx.enter_context(tc.tile_pool(name="feats", bufs=1))
        xload = ctx.enter_context(tc.tile_pool(name="xload", bufs=4))
        xwork = ctx.enter_context(tc.tile_pool(name="xwork", bufs=4))
        wload = ctx.enter_context(tc.tile_pool(name="wload", bufs=RAW_PASSES))
        wwork = ctx.enter_context(tc.tile_pool(name="wwork", bufs=3))
        wquant = ctx.enter_context(tc.tile_pool(name="wquant", bufs=3))
        result = ctx.enter_context(tc.tile_pool(name="result", bufs=8))
        psum = ctx.enter_context(tc.psum_pool(name="psum", bufs=8))

        identity = const.tile([P, P], F32)
        make_identity(nc, identity[:])

        ones = const.tile([P, P], BF16)
        nc.vector.memset(ones[:], 1.0)
        bias_row = const.tile([P, 2 * BANK], BF16)
        nc.vector.memset(bias_row[:], 0.0)
        nc.scalar.dma_start(out=bias_row[0:1, 0 : 7 * C_OUT], in_=b0.rearrange("(o n) -> o n", o=1))

        x_codes = {}
        x_scales = {}
        neg_codes = {}
        neg_scales = {}
        loads = []
        load_size = 1
        for weight, first, count, is_complex in orders:
            a = 0
            while a < count:
                n_coeffs = min(load_size, count - a)
                if is_complex:
                    loads.append((first + count + a, n_coeffs))
                loads.append((first + a, n_coeffs))
                a += n_coeffs
                load_size = min(2 * load_size, LOAD_COEFFS)
        for c0, n_coeffs in loads:
            xraw = xload.tile([P, EDGE_TILES * n_coeffs * K_PASS], BF16)
            nc.sync.dma_start(
                out=xraw[:].rearrange("p (t x) -> p t x", t=EDGE_TILES),
                in_=edge_feats[:, c0 : c0 + n_coeffs, :].rearrange("(t p) c k -> p t (c k)", p=P),
            )
            xwords = xraw[:].bitcast(F32)
            for j in range(n_coeffs):
                c = c0 + j
                bank = psum.tile([P, BANK], F32, tag="bank")
                for t in range(EDGE_TILES):
                    for u in range(2):
                        w0 = ((t * n_coeffs + j) * 2 + u) * P
                        s = 2 * t + u
                        nc.tensor.transpose(bank[:, s * P : (s + 1) * P], xwords[:, w0 : w0 + P], identity[:])
                xg = xwork.tile([P, EDGE_TILES * P * PACK], BF16, align_bytes=64)
                nc.scalar.copy(
                    out=xg[:].bitcast(F32).rearrange("p (t e u) -> p t e u", t=EDGE_TILES, u=2),
                    in_=bank[:].rearrange("p (t u e) -> p t e u", t=EDGE_TILES, u=2),
                )
                if c in imaginary:
                    xn = xwork.tile([P, EDGE_TILES * P * PACK], BF16, align_bytes=64)
                    nc.vector.tensor_scalar_mul(out=xn[:], in0=xg[:], scalar1=-1.0)
                x_codes[c] = feats.tile([P, EDGE_TILES * P], U32, name="xq%d" % c, align_bytes=64)
                x_scales[c] = feats.tile([P, EDGE_TILES * P], U8, name="xs%d" % c, align_bytes=64)
                nc.vector.quantize_mx(out=x_codes[c][:].bitcast(FP8X4), scales=x_scales[c][:], in_=xg[:])
                if c in imaginary:
                    neg_codes[c] = feats.tile([P, EDGE_TILES * P], U32, name="nq%d" % c, align_bytes=64)
                    neg_scales[c] = feats.tile([P, EDGE_TILES * P], U8, name="ns%d" % c, align_bytes=64)
                    nc.vector.quantize_mx(out=neg_codes[c][:].bitcast(FP8X4), scales=neg_scales[c][:], in_=xn[:])

        bias = const.tile([P, 2 * BANK], F32)
        for a in range(0, 2 * BANK, BANK):
            spread = psum.tile([P, BANK], F32, tag="bank")
            nc.tensor.matmul(spread[:], lhsT=ones[:], rhs=bias_row[:, a : a + BANK], start=True, stop=True)
            nc.scalar.copy(out=bias[:, a : a + BANK], in_=spread[:])

        raw = {}
        grouped = {}
        w_codes = {}
        w_scales = {}
        acc = {}
        stores = []

        def load(i):
            m, g = passes[i]
            weight = orders[m][0]
            raw[i] = wload.tile([P, PACK, weight.shape[1]], BF16, name="wraw%d" % i, tag="wraw")
            nc.sync.dma_start(
                out=raw[i][:].rearrange("p (u e) n -> p u e n", u=2),
                in_=weight[g * K_PASS : (g + 1) * K_PASS, :].rearrange("(u p e) n -> p u e n", u=2, e=2),
            )

        def regroup(i):
            n_cols = orders[passes[i][0]][0].shape[1]
            split = n_cols // 2 - VECTOR_FEWER
            grouped[i] = wwork.tile([P, n_cols, PACK], BF16, name="wg%d" % i, tag="wg", align_bytes=64)
            nc.vector.tensor_copy(
                out=grouped[i][:, 0:split, :].rearrange("p (c i) t -> p c t i", i=4),
                in_=raw[i][:, :, 0:split].rearrange("p t (c i) -> p c t i", i=4),
            )
            nc.scalar.copy(
                out=grouped[i][:, split:n_cols, :].rearrange("p (c i) t -> p c t i", i=4),
                in_=raw[i][:, :, split:n_cols].rearrange("p t (c i) -> p c t i", i=4),
            )

        def quantise(i):
            n_cols = orders[passes[i][0]][0].shape[1]
            w_codes[i] = wquant.tile([P, n_cols], U32, name="wq%d" % i, tag="wq", align_bytes=64)
            w_scales[i] = wquant.tile([P, n_cols], U8, name="ws%d" % i, tag="ws", align_bytes=64)
            for a, w in power_of_two_pieces(n_cols, 1024):
                nc.vector.quantize_mx(
                    out=w_codes[i][:, a : a + w].bitcast(FP8X4),
                    scales=w_scales[i][:, a : a + w],
                    in_=grouped[i][:, a : a + w, :].rearrange("p w j -> p (w j)"),
                )

        def multiply(i):
            m, g = passes[i]
            weight, first, count, is_complex = orders[m]
            width = count * C_OUT
            re = first + g
            im = first + count + g
            for t in range(EDGE_TILES):
                edges = slice(t * P, (t + 1) * P)
                for part in range(2 if is_complex else 1):
                    if not is_complex:
                        terms = [(x_codes[re], x_scales[re], 0)]
                    elif part == 0:
                        terms = [(x_codes[re], x_scales[re], 0), (neg_codes[im], neg_scales[im], width)]
                    else:
                        terms = [(x_codes[im], x_scales[im], 0), (x_codes[re], x_scales[re], width)]
                    for a, w in power_of_two_pieces(width, BANK):
                        if g == 0:
                            acc[(m, t, part, a)] = psum.tile([P, BANK], F32, tag="bank", name="acc_%d_%d_%d_%d" % (m, t, part, a))
                        for k, (codes, scales, offset) in enumerate(terms):
                            cols = slice(offset + a, offset + a + w)
                            nc.tensor.matmul_mx(
                                out=acc[(m, t, part, a)][:, 0:w],
                                lhsT=codes[:, edges].bitcast(FP8X4),
                                lhsT_scale=scales[:, edges],
                                rhs=w_codes[i][:, cols].bitcast(FP8X4),
                                rhs_scale=w_scales[i][:, cols],
                                start=(g == 0 and k == 0),
                                stop=(g == count - 1 and k == len(terms) - 1),
                            )

        def finish(m):
            weight, first, count, is_complex = orders[m]
            width = count * C_OUT
            for t in range(EDGE_TILES):
                for part in range(2 if is_complex else 1):
                    stage = result.tile([P, width], F32)
                    for a, w in power_of_two_pieces(width, BANK):
                        if not is_complex:
                            nc.vector.tensor_tensor(
                                out=stage[:, a : a + w],
                                in0=acc[(m, t, part, a)][:, 0:w],
                                in1=bias[:, a : a + w],
                                op=mybir.AluOpType.add,
                            )
                        elif part == 0:
                            nc.scalar.copy(out=stage[:, a : a + w], in_=acc[(m, t, part, a)][:, 0:w])
                        else:
                            nc.vector.tensor_copy(out=stage[:, a : a + w], in_=acc[(m, t, part, a)][:, 0:w])
                    c0 = first + part * count
                    stores.append((out[t * P : (t + 1) * P, c0 : c0 + count, :].rearrange("p c d -> p (c d)"), stage))

        for i in range(RAW_PASSES):
            load(i)
        for s in range(len(passes) + 2):
            if s < len(passes):
                regroup(s)
            if s + RAW_PASSES < len(passes):
                load(s + RAW_PASSES)
            if 1 <= s <= len(passes):
                quantise(s - 1)
            if s >= 2:
                m, g = passes[s - 2]
                if g == orders[m][2] - 1:
                    finish(m)
            if 1 <= s <= len(passes):
                multiply(s - 1)
            if s + RAW_PASSES >= len(passes) - 1:
                for target, stage in stores:
                    nc.sync.dma_start(out=target, in_=stage[:])
                stores = []
